import numpy as np
import ml_dtypes


def mxq(x, axis, fmt="e4m3"):
    dtype, down = {"e4m3": (ml_dtypes.float8_e4m3fn, 7), "e5m2": (ml_dtypes.float8_e5m2, 14)}[fmt]
    v = np.moveaxis(np.asarray(x, np.float32).astype(ml_dtypes.bfloat16).astype(np.float64), axis, -1)
    blocks = v.reshape(v.shape[:-1] + (-1, 32))
    amax = np.abs(blocks).max(-1, keepdims=True)
    byte = np.maximum(np.where(amax > 0, np.frexp(amax)[1] - 1 + 127, 0) - down, 1)
    scale = np.exp2(byte - 127.0)
    codes = (blocks / scale).astype(np.float32).astype(dtype).astype(np.float64)
    return np.moveaxis((codes * scale).reshape(v.shape), -1, axis)


WIDE = False


def mx_kscale(k):
    if not WIDE:
        return np.ones(k)
    levels = np.array([10, -10, 5, -5, 0])
    a = np.random.permutation(np.resize(levels, k // 512 * 4)).reshape(k // 512, 4)
    idx = np.arange(k)
    return np.exp2(a[idx // 512, idx % 128 // 32])


BF16 = ml_dtypes.bfloat16


def bf(x):
    return np.asarray(x, np.float32).astype(BF16)


def f64(x):
    return np.asarray(x).astype(np.float64)


B, T, N, D, H = 2, 2, 512, 512, 4


def setup_inputs():
    t = mx_kscale(D)
    return {"adj": bf(np.random.uniform(size=(N, N)) * 16.0 / N),
            "query": bf(np.random.standard_normal((B, T, N, D)) * 0.8 * t),
            "Wt": bf(np.random.standard_normal((D, D)) * 10.0 / np.sqrt(D) / t),
            "bt": bf(np.random.standard_normal(D) * 0.2)}


def reference(adj, query, Wt, bt):
    A = f64(adj) + np.eye(N)
    nadj = A / A.sum(1, keepdims=True)
    gq = mxq(nadj, 1, "e4m3") @ mxq(f64(query), 2, "e4m3")
    return np.maximum((mxq(gq, 3, "e4m3") @ mxq(f64(Wt), 1, "e4m3").T) + f64(bt), 0.0)

@@ -1,0 +1,168 @@
+import concourse.mybir as mybir
+from concourse.masks import make_identity
+
+FP8X4 = mybir.dt.float8_e4m3fn_x4
+BF16 = mybir.dt.bfloat16
+F32 = mybir.dt.float32
+U32 = mybir.dt.uint32
+U8 = mybir.dt.uint8
+ALU = mybir.AluOpType
+ACT = mybir.ActivationFunctionType
+
+P = 128
+PACK = 4
+NODES = 512
+FEATS = 512
+GRAPHS = 4
+TILES = NODES // P
+
+FLOPS = 2 * 2 * GRAPHS * NODES * NODES * FEATS
+
+
+def tile_gatedspatialattentionlayer_pc_kernel(tc, adj, query, Wt, bt, out):
+    nc = tc.nc
+    query_rows = query.flatten_outer_dims()
+    out_rows = out.flatten_outer_dims()
+
+    with tc.tile_pool(name="keep", bufs=1) as keep, tc.tile_pool(
+        name="work", bufs=4
+    ) as work, tc.psum_pool(name="psum", bufs=2) as psum:
+        adj_sb = keep.tile([P, TILES, NODES], BF16)
+        query_sb = keep.tile([P, GRAPHS, PACK, FEATS], BF16)
+        wt_sb = keep.tile([P, TILES, FEATS], BF16)
+
+        def load_query(g):
+            nc.sync.dma_start(
+                out=query_sb[:, g, :, :],
+                in_=query_rows[g * NODES : (g + 1) * NODES, :].rearrange(
+                    "(j p) d -> p j d", p=P
+                ),
+            )
+
+        for i in range(TILES):
+            nc.sync.dma_start(out=adj_sb[:, i, :], in_=adj[i * P : (i + 1) * P, :])
+        load_query(0)
+        nc.sync.dma_start(out=wt_sb[:], in_=Wt.rearrange("(i p) d -> p i d", p=P))
+        for g in range(1, GRAPHS):
+            load_query(g)
+
+        eye = keep.tile([P, TILES, NODES], BF16)
+        nc.vector.memset(eye[:], 0.0)
+        for i in range(TILES):
+            make_identity(nc, eye[:, i, i * P : (i + 1) * P], nomemset=True)
+        ident = eye[:, 0, 0:P]
+
+        bias_rows = keep.tile([P, FEATS], BF16)
+        nc.vector.memset(bias_rows[:], 0.0)
+        nc.scalar.dma_start(out=bias_rows[0:1, :], in_=bt.rearrange("(o f) -> o f", o=1))
+        ones = keep.tile([P, P], BF16)
+        nc.vector.memset(ones[:], 1.0)
+        bias_bank = psum.tile([P, FEATS], F32, tag="out_bank", bufs=3)
+        nc.tensor.matmul(out=bias_bank[:], lhsT=ones[:], rhs=bias_rows[:], start=True, stop=True)
+        bias_sb = keep.tile([P, FEATS], F32)
+        nc.scalar.copy(out=bias_sb[:], in_=bias_bank[:])
+
+        a_grouped = keep.tile([P, TILES, P, PACK], BF16, align_bytes=64)
+        a_codes = keep.tile([P, NODES], U32, align_bytes=64)
+        a_scales = keep.tile([P, NODES], U8, align_bytes=64)
+        for i in range(TILES):
+            cols = slice(i * P, (i + 1) * P)
+            a_f32 = work.tile([P, NODES], F32, tag="a_f32")
+            row_sum = work.tile([P, 1], F32, tag="row_sum")
+            nc.vector.scalar_tensor_tensor(
+                out=a_f32[:],
+                in0=adj_sb[:, i, :],
+                scalar=1.0,
+                in1=eye[:, i, :],
+                op0=ALU.mult,
+                op1=ALU.add,
+                accum_out=row_sum[:],
+            )
+            inv_sum = work.tile([P, 1], F32, tag="inv_sum")
+            nc.vector.reciprocal(out=inv_sum[:], in_=row_sum[:])
+            nadj = work.tile([P, NODES], BF16, tag="nadj")
+            nc.scalar.activation(out=nadj[:], in_=a_f32[:], func=ACT.Copy, scale=inv_sum[:, 0:1])
+            at = psum.tile([P, PACK, P], BF16, tag="transposed")
+            for j in range(PACK):
+                nc.tensor.transpose(out=at[:, j, :], in_=nadj[:, j * P : (j + 1) * P], identity=ident)
+            nc.scalar.copy(out=a_grouped[:, i, :, :], in_=at[:].rearrange("p j n -> p n j"))
+            nc.vector.quantize_mx(
+                out=a_codes[:, cols].bitcast(FP8X4),
+                scales=a_scales[:, cols],
+                in_=a_grouped[:, i, :, :].rearrange("p n j -> p (n j)"),
+            )
+
+        q_codes = keep.tile([P, GRAPHS, FEATS], U32, align_bytes=64)
+        q_scales = keep.tile([P, GRAPHS, FEATS], U8, align_bytes=64)
+
+        def quantise_query(g):
+            q_grouped = work.tile([P, FEATS, PACK], BF16, tag="q_grouped", align_bytes=64)
+            nc.vector.tensor_copy(
+                out=q_grouped[:].rearrange("p (c i) j -> p c j i", i=4),
+                in_=query_sb[:, g, :, :].rearrange("p j (c i) -> p c j i", i=4),
+            )
+            nc.vector.quantize_mx(
+                out=q_codes[:, g, :].bitcast(FP8X4),
+                scales=q_scales[:, g, :],
+                in_=q_grouped[:].rearrange("p d j -> p (d j)"),
+            )
+
+        quantise_query(0)
+
+        w_grouped = keep.tile([P, TILES, P, PACK], BF16, align_bytes=64)
+        w_codes = keep.tile([P, FEATS], U32, align_bytes=64)
+        w_scales = keep.tile([P, FEATS], U8, align_bytes=64)
+        for i in range(TILES):
+            wt_t = psum.tile([P, PACK, P], BF16, tag="transposed")
+            for j in range(PACK):
+                nc.tensor.transpose(
+                    out=wt_t[:, j, :], in_=wt_sb[:, i, j * P : (j + 1) * P], identity=ident
+                )
+            nc.scalar.copy(out=w_grouped[:, i, :, :], in_=wt_t[:].rearrange("p j o -> p o j"))
+        nc.vector.quantize_mx(
+            out=w_codes[:].bitcast(FP8X4),
+            scales=w_scales[:],
+            in_=w_grouped[:].rearrange("p i o j -> p (i o j)"),
+        )
+
+        for g in range(GRAPHS):
+            if g > 0:
+                quantise_query(g)
+            for i in range(TILES):
+                cols = slice(i * P, (i + 1) * P)
+                gq_bank = psum.tile([P, PACK, P], F32, tag="gq_bank", bufs=3)
+                for j in range(PACK):
+                    nc.tensor.matmul_mx(
+                        out=gq_bank[:, j, :],
+                        lhsT=q_codes[:, g, j * P : (j + 1) * P].bitcast(FP8X4),
+                        lhsT_scale=q_scales[:, g, j * P : (j + 1) * P],
+                        rhs=a_codes[:, cols].bitcast(FP8X4),
+                        rhs_scale=a_scales[:, cols],
+                        start=True,
+                        stop=True,
+                    )
+                gq_grouped = work.tile([P, P, PACK], BF16, tag="gq_grouped", align_bytes=64)
+                nc.scalar.copy(out=gq_grouped[:], in_=gq_bank[:].rearrange("p j n -> p n j"))
+                gq_codes = work.tile([P, P], U32, tag="gq_codes", align_bytes=64)
+                gq_scales = work.tile([P, P], U8, tag="gq_scales", align_bytes=64)
+                nc.vector.quantize_mx(
+                    out=gq_codes[:].bitcast(FP8X4),
+                    scales=gq_scales[:],
+                    in_=gq_grouped[:].rearrange("p n j -> p (n j)"),
+                )
+                out_bank = psum.tile([P, FEATS], F32, tag="out_bank", bufs=3)
+                nc.tensor.matmul_mx(
+                    out=out_bank[:],
+                    lhsT=gq_codes[:].bitcast(FP8X4),
+                    lhsT_scale=gq_scales[:],
+                    rhs=w_codes[:].bitcast(FP8X4),
+                    rhs_scale=w_scales[:],
+                    start=True,
+                    stop=True,
+                )
+                biased = work.tile([P, FEATS], F32, tag="biased")
+                nc.vector.tensor_tensor(out=biased[:], in0=out_bank[:], in1=bias_sb[:], op=ALU.add)
+                result = work.tile([P, FEATS], F32, tag="result")
+                nc.scalar.activation(out=result[:], in_=biased[:], func=ACT.Relu)
+                first_row = g * NODES + i * P
+                nc.sync.dma_start(out=out_rows[first_row : first_row + P, :], in_=result[:])

@@ -19,14 +19,21 @@ TILES = NODES // P
 FLOPS = 2 * 2 * GRAPHS * NODES * NODES * FEATS
 
 
+UNITS = GRAPHS * TILES
+QUANTISE_LAG = 3
+BIAS_LAG = 4
+RELU_LAG = 5
+
+
 def tile_gatedspatialattentionlayer_pc_kernel(tc, adj, query, Wt, bt, out):
     nc = tc.nc
     query_rows = query.flatten_outer_dims()
     out_rows = out.flatten_outer_dims()
 
     with tc.tile_pool(name="keep", bufs=1) as keep, tc.tile_pool(
-        name="work", bufs=4
-    ) as work, tc.psum_pool(name="psum", bufs=2) as psum:
+        name="work", bufs=6
+    ) as work, tc.psum_pool(name="psum", bufs=8) as psum, tc.manual_schedule():
+
         adj_sb = keep.tile([P, TILES, NODES], BF16)
         query_sb = keep.tile([P, GRAPHS, PACK, FEATS], BF16)
         wt_sb = keep.tile([P, TILES, FEATS], BF16)
@@ -41,32 +48,30 @@ def tile_gatedspatialattentionlayer_pc_kernel(tc, adj, query, Wt, bt, out):
 
         for i in range(TILES):
             nc.sync.dma_start(out=adj_sb[:, i, :], in_=adj[i * P : (i + 1) * P, :])
+        bias_rows = keep.tile([P, FEATS], BF16)
+        nc.vector.memset(bias_rows[:], 0.0)
+        nc.sync.dma_start(out=bias_rows[0:1, :], in_=bt.rearrange("(o f) -> o f", o=1))
         load_query(0)
+        load_query(1)
         nc.sync.dma_start(out=wt_sb[:], in_=Wt.rearrange("(i p) d -> p i d", p=P))
-        for g in range(1, GRAPHS):
-            load_query(g)
+        load_query(2)
+        load_query(3)
 
+        ones = keep.tile([P, P], BF16)
+        nc.vector.memset(ones[:], 1.0)
+        ident = keep.tile([P, P], BF16)
+        make_identity(nc, ident[:])
         eye = keep.tile([P, TILES, NODES], BF16)
         nc.vector.memset(eye[:], 0.0)
         for i in range(TILES):
-            make_identity(nc, eye[:, i, i * P : (i + 1) * P], nomemset=True)
-        ident = eye[:, 0, 0:P]
-
-        bias_rows = keep.tile([P, FEATS], BF16)
-        nc.vector.memset(bias_rows[:], 0.0)
-        nc.scalar.dma_start(out=bias_rows[0:1, :], in_=bt.rearrange("(o f) -> o f", o=1))
-        ones = keep.tile([P, P], BF16)
-        nc.vector.memset(ones[:], 1.0)
-        bias_bank = psum.tile([P, FEATS], F32, tag="out_bank", bufs=3)
-        nc.tensor.matmul(out=bias_bank[:], lhsT=ones[:], rhs=bias_rows[:], start=True, stop=True)
-        bias_sb = keep.tile([P, FEATS], F32)
-        nc.scalar.copy(out=bias_sb[:], in_=bias_bank[:])
+            nc.vector.tensor_copy(out=eye[:, i, i * P : (i + 1) * P], in_=ident[:])
 
         a_grouped = keep.tile([P, TILES, P, PACK], BF16, align_bytes=64)
         a_codes = keep.tile([P, NODES], U32, align_bytes=64)
         a_scales = keep.tile([P, NODES], U8, align_bytes=64)
-        for i in range(TILES):
-            cols = slice(i * P, (i + 1) * P)
+        a_banks = []
+
+        def normalise_and_transpose(i):
             a_f32 = work.tile([P, NODES], F32, tag="a_f32")
             row_sum = work.tile([P, 1], F32, tag="row_sum")
             nc.vector.scalar_tensor_tensor(
@@ -82,87 +87,145 @@ def tile_gatedspatialattentionlayer_pc_kernel(tc, adj, query, Wt, bt, out):
             nc.vector.reciprocal(out=inv_sum[:], in_=row_sum[:])
             nadj = work.tile([P, NODES], BF16, tag="nadj")
             nc.scalar.activation(out=nadj[:], in_=a_f32[:], func=ACT.Copy, scale=inv_sum[:, 0:1])
-            at = psum.tile([P, PACK, P], BF16, tag="transposed")
+            a_bank = psum.tile([P, PACK, P], BF16, tag="bank", name="a_bank")
             for j in range(PACK):
-                nc.tensor.transpose(out=at[:, j, :], in_=nadj[:, j * P : (j + 1) * P], identity=ident)
-            nc.scalar.copy(out=a_grouped[:, i, :, :], in_=at[:].rearrange("p j n -> p n j"))
-            nc.vector.quantize_mx(
-                out=a_codes[:, cols].bitcast(FP8X4),
-                scales=a_scales[:, cols],
-                in_=a_grouped[:, i, :, :].rearrange("p n j -> p (n j)"),
+                nc.tensor.transpose(
+                    out=a_bank[:, j, :], in_=nadj[:, j * P : (j + 1) * P], identity=ident[:]
+                )
+            a_banks.append(a_bank)
+
+        def group_nadj(i):
+            nc.scalar.copy(
+                out=a_grouped[:, i, :, :], in_=a_banks[i][:].rearrange("p j n -> p n j")
             )
 
-        q_codes = keep.tile([P, GRAPHS, FEATS], U32, align_bytes=64)
-        q_scales = keep.tile([P, GRAPHS, FEATS], U8, align_bytes=64)
-
-        def quantise_query(g):
-            q_grouped = work.tile([P, FEATS, PACK], BF16, tag="q_grouped", align_bytes=64)
-            nc.vector.tensor_copy(
-                out=q_grouped[:].rearrange("p (c i) j -> p c j i", i=4),
-                in_=query_sb[:, g, :, :].rearrange("p j (c i) -> p c j i", i=4),
-            )
-            nc.vector.quantize_mx(
-                out=q_codes[:, g, :].bitcast(FP8X4),
-                scales=q_scales[:, g, :],
-                in_=q_grouped[:].rearrange("p d j -> p (d j)"),
-            )
-
-        quantise_query(0)
+        for i in range(TILES + 1):
+            if i < TILES:
+                normalise_and_transpose(i)
+            if i > 0:
+                group_nadj(i - 1)
 
         w_grouped = keep.tile([P, TILES, P, PACK], BF16, align_bytes=64)
         w_codes = keep.tile([P, FEATS], U32, align_bytes=64)
         w_scales = keep.tile([P, FEATS], U8, align_bytes=64)
+        w_banks = []
         for i in range(TILES):
-            wt_t = psum.tile([P, PACK, P], BF16, tag="transposed")
+            w_bank = psum.tile([P, PACK, P], BF16, tag="bank", name="w_bank")
             for j in range(PACK):
                 nc.tensor.transpose(
-                    out=wt_t[:, j, :], in_=wt_sb[:, i, j * P : (j + 1) * P], identity=ident
+                    out=w_bank[:, j, :], in_=wt_sb[:, i, j * P : (j + 1) * P], identity=ident[:]
                 )
-            nc.scalar.copy(out=w_grouped[:, i, :, :], in_=wt_t[:].rearrange("p j o -> p o j"))
+            w_banks.append(w_bank)
+
+        bias_bank = psum.tile([P, FEATS], F32, tag="bank")
+        nc.tensor.matmul(out=bias_bank[:], lhsT=ones[:], rhs=bias_rows[:], start=True, stop=True)
+        bias_sb = keep.tile([P, FEATS], F32)
+
+        q_grouped = keep.tile([P, GRAPHS, FEATS, PACK], BF16, align_bytes=64)
+        q_codes = keep.tile([P, GRAPHS, FEATS], U32, align_bytes=64)
+        q_scales = keep.tile([P, GRAPHS, FEATS], U8, align_bytes=64)
+
+        def group_query(g):
+            nc.vector.tensor_copy(
+                out=q_grouped[:, g, :, :].rearrange("p (c i) j -> p c j i", i=4),
+                in_=query_sb[:, g, :, :].rearrange("p j (c i) -> p c j i", i=4),
+            )
+
+        def quantise_query(g):
+            nc.vector.quantize_mx(
+                out=q_codes[:, g, :].bitcast(FP8X4),
+                scales=q_scales[:, g, :],
+                in_=q_grouped[:, g, :, :].rearrange("p d j -> p (d j)"),
+            )
+
+        group_query(0)
+        group_query(1)
+        quantise_query(0)
+        quantise_query(1)
+        nc.vector.quantize_mx(
+            out=a_codes[:].bitcast(FP8X4),
+            scales=a_scales[:],
+            in_=a_grouped[:].rearrange("p i n j -> p (i n j)"),
+        )
+        for i in range(TILES):
+            nc.scalar.copy(out=w_grouped[:, i, :, :], in_=w_banks[i][:].rearrange("p j o -> p o j"))
+        nc.scalar.copy(out=bias_sb[:], in_=bias_bank[:])
+        group_query(2)
         nc.vector.quantize_mx(
             out=w_codes[:].bitcast(FP8X4),
             scales=w_scales[:],
             in_=w_grouped[:].rearrange("p i o j -> p (i o j)"),
         )
 
-        for g in range(GRAPHS):
-            if g > 0:
-                quantise_query(g)
-            for i in range(TILES):
-                cols = slice(i * P, (i + 1) * P)
-                gq_bank = psum.tile([P, PACK, P], F32, tag="gq_bank", bufs=3)
-                for j in range(PACK):
-                    nc.tensor.matmul_mx(
-                        out=gq_bank[:, j, :],
-                        lhsT=q_codes[:, g, j * P : (j + 1) * P].bitcast(FP8X4),
-                        lhsT_scale=q_scales[:, g, j * P : (j + 1) * P],
-                        rhs=a_codes[:, cols].bitcast(FP8X4),
-                        rhs_scale=a_scales[:, cols],
-                        start=True,
-                        stop=True,
-                    )
-                gq_grouped = work.tile([P, P, PACK], BF16, tag="gq_grouped", align_bytes=64)
-                nc.scalar.copy(out=gq_grouped[:], in_=gq_bank[:].rearrange("p j n -> p n j"))
-                gq_codes = work.tile([P, P], U32, tag="gq_codes", align_bytes=64)
-                gq_scales = work.tile([P, P], U8, tag="gq_scales", align_bytes=64)
-                nc.vector.quantize_mx(
-                    out=gq_codes[:].bitcast(FP8X4),
-                    scales=gq_scales[:],
-                    in_=gq_grouped[:].rearrange("p n j -> p (n j)"),
-                )
-                out_bank = psum.tile([P, FEATS], F32, tag="out_bank", bufs=3)
+        gq_banks, gq_groupeds, out_banks, biaseds = {}, {}, {}, {}
+
+        def first_product(u):
+            g, cols = u // TILES, slice((u % TILES) * P, (u % TILES + 1) * P)
+            gq_bank = psum.tile([P, PACK, P], F32, tag="bank", name="gq_bank")
+            for j in range(PACK):
                 nc.tensor.matmul_mx(
-                    out=out_bank[:],
-                    lhsT=gq_codes[:].bitcast(FP8X4),
-                    lhsT_scale=gq_scales[:],
-                    rhs=w_codes[:].bitcast(FP8X4),
-                    rhs_scale=w_scales[:],
+                    out=gq_bank[:, j, :],
+                    lhsT=q_codes[:, g, j * P : (j + 1) * P].bitcast(FP8X4),
+                    lhsT_scale=q_scales[:, g, j * P : (j + 1) * P],
+                    rhs=a_codes[:, cols].bitcast(FP8X4),
+                    rhs_scale=a_scales[:, cols],
                     start=True,
                     stop=True,
                 )
-                biased = work.tile([P, FEATS], F32, tag="biased")
-                nc.vector.tensor_tensor(out=biased[:], in0=out_bank[:], in1=bias_sb[:], op=ALU.add)
-                result = work.tile([P, FEATS], F32, tag="result")
-                nc.scalar.activation(out=result[:], in_=biased[:], func=ACT.Relu)
-                first_row = g * NODES + i * P
-                nc.sync.dma_start(out=out_rows[first_row : first_row + P, :], in_=result[:])
+            gq_banks[u] = gq_bank
+
+        def round_gq(u):
+            gq_grouped = work.tile([P, P, PACK], BF16, tag="gq_grouped", align_bytes=64)
+            nc.scalar.copy(out=gq_grouped[:], in_=gq_banks[u][:].rearrange("p j n -> p n j"))
+            gq_groupeds[u] = gq_grouped
+
+        def second_product(u):
+            gq_codes = work.tile([P, P], U32, tag="gq_codes", align_bytes=64)
+            gq_scales = work.tile([P, P], U8, tag="gq_scales", align_bytes=64)
+            nc.vector.quantize_mx(
+                out=gq_codes[:].bitcast(FP8X4),
+                scales=gq_scales[:],
+                in_=gq_groupeds[u][:].rearrange("p n j -> p (n j)"),
+            )
+            out_bank = psum.tile([P, FEATS], F32, tag="bank", name="out_bank")
+            nc.tensor.matmul_mx(
+                out=out_bank[:],
+                lhsT=gq_codes[:].bitcast(FP8X4),
+                lhsT_scale=gq_scales[:],
+                rhs=w_codes[:].bitcast(FP8X4),
+                rhs_scale=w_scales[:],
+                start=True,
+                stop=True,
+            )
+            out_banks[u] = out_bank
+
+        def add_bias(u):
+            biased = work.tile([P, FEATS], F32, tag="biased")
+            nc.vector.tensor_tensor(out=biased[:], in0=out_banks[u][:], in1=bias_sb[:], op=ALU.add)
+            biaseds[u] = biased
+
+        def relu_and_store(u):
+            result = work.tile([P, FEATS], F32, tag="result")
+            if u % TILES == TILES - 1:
+                nc.vector.tensor_scalar_max(out=result[:], in0=biaseds[u][:], scalar1=0.0)
+            else:
+                nc.scalar.activation(out=result[:], in_=biaseds[u][:], func=ACT.Relu)
+            nc.sync.dma_start(out=out_rows[u * P : (u + 1) * P, :], in_=result[:])
+
+        first_product(0)
+        for step in range(UNITS + RELU_LAG):
+            g, i = step // TILES, step % TILES
+            if step + 1 < UNITS:
+                first_product(step + 1)
+            if step < UNITS:
+                round_gq(step)
+            if 0 <= step - QUANTISE_LAG < UNITS:
+                second_product(step - QUANTISE_LAG)
+            if i == 1 and g + 3 < GRAPHS:
+                group_query(g + 3)
+            if 0 <= step - BIAS_LAG < UNITS:
+                add_bias(step - BIAS_LAG)
+            if i == 0 and g + 2 < GRAPHS:
+                quantise_query(g + 2)
+            if 0 <= step - RELU_LAG < UNITS:
+                relu_and_store(step - RELU_LAG)

@@ -48,17 +48,14 @@ def tile_gatedspatialattentionlayer_pc_kernel(tc, adj, query, Wt, bt, out):
 
         for i in range(TILES):
             nc.sync.dma_start(out=adj_sb[:, i, :], in_=adj[i * P : (i + 1) * P, :])
-        bias_rows = keep.tile([P, FEATS], BF16)
-        nc.vector.memset(bias_rows[:], 0.0)
-        nc.sync.dma_start(out=bias_rows[0:1, :], in_=bt.rearrange("(o f) -> o f", o=1))
         load_query(0)
         load_query(1)
         nc.sync.dma_start(out=wt_sb[:], in_=Wt.rearrange("(i p) d -> p i d", p=P))
         load_query(2)
         load_query(3)
+        bias_sb = keep.tile([P, FEATS], BF16)
+        nc.sync.dma_start(out=bias_sb[:], in_=bt.partition_broadcast(P))
 
-        ones = keep.tile([P, P], BF16)
-        nc.vector.memset(ones[:], 1.0)
         ident = keep.tile([P, P], BF16)
         make_identity(nc, ident[:])
         eye = keep.tile([P, TILES, NODES], BF16)
@@ -117,10 +114,6 @@ def tile_gatedspatialattentionlayer_pc_kernel(tc, adj, query, Wt, bt, out):
                 )
             w_banks.append(w_bank)
 
-        bias_bank = psum.tile([P, FEATS], F32, tag="bank")
-        nc.tensor.matmul(out=bias_bank[:], lhsT=ones[:], rhs=bias_rows[:], start=True, stop=True)
-        bias_sb = keep.tile([P, FEATS], F32)
-
         q_grouped = keep.tile([P, GRAPHS, FEATS, PACK], BF16, align_bytes=64)
         q_codes = keep.tile([P, GRAPHS, FEATS], U32, align_bytes=64)
         q_scales = keep.tile([P, GRAPHS, FEATS], U8, align_bytes=64)
@@ -149,7 +142,6 @@ def tile_gatedspatialattentionlayer_pc_kernel(tc, adj, query, Wt, bt, out):
         )
         for i in range(TILES):
             nc.scalar.copy(out=w_grouped[:, i, :, :], in_=w_banks[i][:].rearrange("p j o -> p o j"))
-        nc.scalar.copy(out=bias_sb[:], in_=bias_bank[:])
         group_query(2)
         nc.vector.quantize_mx(
             out=w_codes[:].bitcast(FP8X4),

@@ -40,9 +40,9 @@ def tile_gatedspatialattentionlayer_pc_kernel(tc, adj, query, Wt, bt, out):
 
         def load_query(g):
             nc.sync.dma_start(
-                out=query_sb[:, g, :, :],
+                out=query_sb[:, g, :, :].rearrange("p (u e) d -> p u (e d)", u=2),
                 in_=query_rows[g * NODES : (g + 1) * NODES, :].rearrange(
-                    "(j p) d -> p j d", p=P
+                    "(u p e) d -> p u (e d)", u=2, e=2
                 ),
             )
 
@@ -58,6 +58,8 @@ def tile_gatedspatialattentionlayer_pc_kernel(tc, adj, query, Wt, bt, out):
 
         ident = keep.tile([P, P], BF16)
         make_identity(nc, ident[:])
+        ident_f32 = keep.tile([P, P], F32)
+        make_identity(nc, ident_f32[:])
         eye = keep.tile([P, TILES, NODES], BF16)
         nc.vector.memset(eye[:], 0.0)
         for i in range(TILES):
@@ -84,16 +86,21 @@ def tile_gatedspatialattentionlayer_pc_kernel(tc, adj, query, Wt, bt, out):
             nc.vector.reciprocal(out=inv_sum[:], in_=row_sum[:])
             nadj = work.tile([P, NODES], BF16, tag="nadj")
             nc.scalar.activation(out=nadj[:], in_=a_f32[:], func=ACT.Copy, scale=inv_sum[:, 0:1])
-            a_bank = psum.tile([P, PACK, P], BF16, tag="bank", name="a_bank")
-            for j in range(PACK):
+            a_bank = psum.tile([P, 2, P], F32, tag="bank", name="a_bank")
+            nadj_words = nadj[:].bitcast(F32)
+            for u in range(2):
                 nc.tensor.transpose(
-                    out=a_bank[:, j, :], in_=nadj[:, j * P : (j + 1) * P], identity=ident[:]
+                    out=a_bank[:, u, :], in_=nadj_words[:, u * P : (u + 1) * P], identity=ident_f32[:]
                 )
             a_banks.append(a_bank)
 
         def group_nadj(i):
             nc.scalar.copy(
-                out=a_grouped[:, i, :, :], in_=a_banks[i][:].rearrange("p j n -> p n j")
+                out=a_grouped[:, i, :, :]
+                .rearrange("p n j -> p (n j)")
+                .bitcast(F32)
+                .rearrange("p (n u) -> p n u", u=2),
+                in_=a_banks[i][:].rearrange("p u n -> p n u"),
             )
 
         for i in range(TILES + 1):
@@ -107,10 +114,11 @@ def tile_gatedspatialattentionlayer_pc_kernel(tc, adj, query, Wt, bt, out):
         w_scales = keep.tile([P, FEATS], U8, align_bytes=64)
         w_banks = []
         for i in range(TILES):
-            w_bank = psum.tile([P, PACK, P], BF16, tag="bank", name="w_bank")
-            for j in range(PACK):
+            w_bank = psum.tile([P, 2, P], F32, tag="bank", name="w_bank")
+            wt_words = wt_sb[:, i, :].bitcast(F32)
+            for u in range(2):
                 nc.tensor.transpose(
-                    out=w_bank[:, j, :], in_=wt_sb[:, i, j * P : (j + 1) * P], identity=ident[:]
+                    out=w_bank[:, u, :], in_=wt_words[:, u * P : (u + 1) * P], identity=ident_f32[:]
                 )
             w_banks.append(w_bank)
 
@@ -120,8 +128,8 @@ def tile_gatedspatialattentionlayer_pc_kernel(tc, adj, query, Wt, bt, out):
 
         def group_query(g):
             nc.vector.tensor_copy(
-                out=q_grouped[:, g, :, :].rearrange("p (c i) j -> p c j i", i=4),
-                in_=query_sb[:, g, :, :].rearrange("p j (c i) -> p c j i", i=4),
+                out=q_grouped[:, g, :, :].rearrange("p (e c) j -> p e c j", e=2),
+                in_=query_sb[:, g, :, :].rearrange("p j (c e) -> p e c j", e=2),
             )
 
         def quantise_query(g):
@@ -131,18 +139,48 @@ def tile_gatedspatialattentionlayer_pc_kernel(tc, adj, query, Wt, bt, out):
                 in_=q_grouped[:, g, :, :].rearrange("p d j -> p (d j)"),
             )
 
+        i_banks = {}
+
+        def interleave_on_tensor(g):
+            for e in range(2):
+                i_bank = psum.tile([P, 2, P * PACK], BF16, tag="bank", name="i_bank")
+                for u in range(2):
+                    nc.tensor.matmul(
+                        out=i_bank[:, u, :].rearrange("p (q j) -> p q j", j=PACK),
+                        lhsT=ident[:],
+                        rhs=query_sb[:, g, :, 2 * P * u + e : 2 * P * (u + 1) : 2].rearrange(
+                            "p j q -> p q j"
+                        ),
+                        start=True,
+                        stop=True,
+                    )
+                i_banks[(g, e)] = i_bank
+
+        def fetch_interleaved(g, e):
+            nc.scalar.copy(
+                out=q_grouped[:, g, 2 * P * e : 2 * P * (e + 1), :]
+                .rearrange("p c j -> p (c j)")
+                .bitcast(F32),
+                in_=i_banks[(g, e)][:].rearrange("p u c -> p (u c)").bitcast(F32),
+            )
+
         group_query(0)
-        group_query(1)
+        interleave_on_tensor(1)
         quantise_query(0)
-        quantise_query(1)
         nc.vector.quantize_mx(
             out=a_codes[:].bitcast(FP8X4),
             scales=a_scales[:],
             in_=a_grouped[:].rearrange("p i n j -> p (i n j)"),
         )
         for i in range(TILES):
-            nc.scalar.copy(out=w_grouped[:, i, :, :], in_=w_banks[i][:].rearrange("p j o -> p o j"))
-        group_query(2)
+            nc.scalar.copy(
+                out=w_grouped[:, i, :, :]
+                .rearrange("p o j -> p (o j)")
+                .bitcast(F32)
+                .rearrange("p (o u) -> p o u", u=2),
+                in_=w_banks[i][:].rearrange("p u o -> p o u"),
+            )
+        fetch_interleaved(1, 0)
         nc.vector.quantize_mx(
             out=w_codes[:].bitcast(FP8X4),
             scales=w_scales[:],
@@ -155,10 +193,11 @@ def tile_gatedspatialattentionlayer_pc_kernel(tc, adj, query, Wt, bt, out):
             g, cols = u // TILES, slice((u % TILES) * P, (u % TILES + 1) * P)
             gq_bank = psum.tile([P, PACK, P], F32, tag="bank", name="gq_bank")
             for j in range(PACK):
+                block = slice((2 * (j % 2) + j // 2) * P, (2 * (j % 2) + j // 2 + 1) * P)
                 nc.tensor.matmul_mx(
                     out=gq_bank[:, j, :],
-                    lhsT=q_codes[:, g, j * P : (j + 1) * P].bitcast(FP8X4),
-                    lhsT_scale=q_scales[:, g, j * P : (j + 1) * P],
+                    lhsT=q_codes[:, g, block].bitcast(FP8X4),
+                    lhsT_scale=q_scales[:, g, block],
                     rhs=a_codes[:, cols].bitcast(FP8X4),
                     rhs_scale=a_scales[:, cols],
                     start=True,
@@ -198,7 +237,7 @@ def tile_gatedspatialattentionlayer_pc_kernel(tc, adj, query, Wt, bt, out):
 
         def relu_and_store(u):
             result = work.tile([P, FEATS], F32, tag="result")
-            if u % TILES == TILES - 1:
+            if u % 2 == 1:
                 nc.vector.tensor_scalar_max(out=result[:], in0=biaseds[u][:], scalar1=0.0)
             else:
                 nc.scalar.activation(out=result[:], in_=biaseds[u][:], func=ACT.Relu)
@@ -209,15 +248,19 @@ def tile_gatedspatialattentionlayer_pc_kernel(tc, adj, query, Wt, bt, out):
             g, i = step // TILES, step % TILES
             if step + 1 < UNITS:
                 first_product(step + 1)
+            if i == 2 and g + 2 < GRAPHS:
+                interleave_on_tensor(g + 2)
             if step < UNITS:
                 round_gq(step)
+            if i == 0 and g + 1 < GRAPHS:
+                fetch_interleaved(g + 1, 1)
+            if i == 3 and g + 2 < GRAPHS:
+                fetch_interleaved(g + 2, 0)
             if 0 <= step - QUANTISE_LAG < UNITS:
                 second_product(step - QUANTISE_LAG)
-            if i == 1 and g + 3 < GRAPHS:
-                group_query(g + 3)
             if 0 <= step - BIAS_LAG < UNITS:
                 add_bias(step - BIAS_LAG)
-            if i == 0 and g + 2 < GRAPHS:
-                quantise_query(g + 2)
+            if i == 1 and g + 1 < GRAPHS:
+                quantise_query(g + 1)
             if 0 <= step - RELU_LAG < UNITS:
                 relu_and_store(step - RELU_LAG)

@@ -15,14 +15,14 @@ NODES = 512
 FEATS = 512
 GRAPHS = 4
 TILES = NODES // P
+UNITS = GRAPHS * TILES
+FLT_MAX = 3.4028234663852886e38
 
 FLOPS = 2 * 2 * GRAPHS * NODES * NODES * FEATS
 
 
-UNITS = GRAPHS * TILES
-QUANTISE_LAG = 3
-BIAS_LAG = 4
-RELU_LAG = 5
+def words(ap, pattern, **sizes):
+    return ap.rearrange("p a b -> p (a b)").bitcast(F32).rearrange(pattern, **sizes)
 
 
 def tile_gatedspatialattentionlayer_pc_kernel(tc, adj, query, Wt, bt, out):
@@ -32,11 +32,13 @@ def tile_gatedspatialattentionlayer_pc_kernel(tc, adj, query, Wt, bt, out):
 
     with tc.tile_pool(name="keep", bufs=1) as keep, tc.tile_pool(
         name="work", bufs=6
-    ) as work, tc.psum_pool(name="psum", bufs=8) as psum, tc.manual_schedule():
-
+    ) as work, tc.psum_pool(name="gq_psum", bufs=2) as gq_psum, tc.psum_pool(
+        name="out_psum", bufs=2
+    ) as out_psum, tc.psum_pool(name="aux_psum", bufs=4) as aux_psum, tc.manual_schedule():
         adj_sb = keep.tile([P, TILES, NODES], BF16)
         query_sb = keep.tile([P, GRAPHS, PACK, FEATS], BF16)
         wt_sb = keep.tile([P, TILES, FEATS], BF16)
+        bias_sb = keep.tile([P, FEATS], BF16)
 
         def load_query(g):
             nc.sync.dma_start(
@@ -49,87 +51,127 @@ def tile_gatedspatialattentionlayer_pc_kernel(tc, adj, query, Wt, bt, out):
         for i in range(TILES):
             nc.sync.dma_start(out=adj_sb[:, i, :], in_=adj[i * P : (i + 1) * P, :])
         load_query(0)
-        load_query(1)
         nc.sync.dma_start(out=wt_sb[:], in_=Wt.rearrange("(i p) d -> p i d", p=P))
+        load_query(1)
+        nc.sync.dma_start(out=bias_sb[:], in_=bt.partition_broadcast(P))
         load_query(2)
         load_query(3)
-        bias_sb = keep.tile([P, FEATS], BF16)
-        nc.sync.dma_start(out=bias_sb[:], in_=bt.partition_broadcast(P))
 
         ident = keep.tile([P, P], BF16)
         make_identity(nc, ident[:])
         ident_f32 = keep.tile([P, P], F32)
         make_identity(nc, ident_f32[:])
-        eye = keep.tile([P, TILES, NODES], BF16)
-        nc.vector.memset(eye[:], 0.0)
-        for i in range(TILES):
-            nc.vector.tensor_copy(out=eye[:, i, i * P : (i + 1) * P], in_=ident[:])
 
+        row_sum = keep.tile([P, TILES], F32)
+        inv_sum = keep.tile([P, TILES], F32)
+        a_diag = keep.tile([P, TILES, P], F32)
         a_grouped = keep.tile([P, TILES, P, PACK], BF16, align_bytes=64)
         a_codes = keep.tile([P, NODES], U32, align_bytes=64)
         a_scales = keep.tile([P, NODES], U8, align_bytes=64)
-        a_banks = []
+        nadjs, a_banks = {}, {}
 
-        def normalise_and_transpose(i):
-            a_f32 = work.tile([P, NODES], F32, tag="a_f32")
-            row_sum = work.tile([P, 1], F32, tag="row_sum")
-            nc.vector.scalar_tensor_tensor(
-                out=a_f32[:],
-                in0=adj_sb[:, i, :],
-                scalar=1.0,
-                in1=eye[:, i, :],
-                op0=ALU.mult,
-                op1=ALU.add,
-                accum_out=row_sum[:],
+        def sum_row(i):
+            unused = work.tile([P, NODES], BF16, tag="unused")
+            nc.scalar.activation(
+                out=unused[:],
+                in_=adj_sb[:, i, :],
+                func=ACT.Copy,
+                bias=1.0 / NODES,
+                accum_out=row_sum[:, i : i + 1],
             )
-            inv_sum = work.tile([P, 1], F32, tag="inv_sum")
-            nc.vector.reciprocal(out=inv_sum[:], in_=row_sum[:])
+
+        def add_self_loops(i):
+            nc.vector.tensor_tensor(
+                out=a_diag[:, i, :], in0=adj_sb[:, i, i * P : (i + 1) * P], in1=ident_f32[:], op=ALU.add
+            )
+
+        def normalise(i):
+            nc.vector.reciprocal(out=inv_sum[:, i : i + 1], in_=row_sum[:, i : i + 1])
             nadj = work.tile([P, NODES], BF16, tag="nadj")
-            nc.scalar.activation(out=nadj[:], in_=a_f32[:], func=ACT.Copy, scale=inv_sum[:, 0:1])
-            a_bank = psum.tile([P, 2, P], F32, tag="bank", name="a_bank")
-            nadj_words = nadj[:].bitcast(F32)
+            nc.vector.tensor_scalar_mul(out=nadj[:], in0=adj_sb[:, i, :], scalar1=inv_sum[:, i : i + 1])
+            nc.vector.tensor_scalar_mul(
+                out=nadj[:, i * P : (i + 1) * P], in0=a_diag[:, i, :], scalar1=inv_sum[:, i : i + 1]
+            )
+            nadjs[i] = nadj
+
+        def transpose_nadj(i):
+            a_bank = aux_psum.tile([P, 2, P], F32, tag="aux", name="a_bank")
+            nadj_words = nadjs[i][:].bitcast(F32)
             for u in range(2):
                 nc.tensor.transpose(
                     out=a_bank[:, u, :], in_=nadj_words[:, u * P : (u + 1) * P], identity=ident_f32[:]
                 )
-            a_banks.append(a_bank)
+            a_banks[i] = a_bank
 
         def group_nadj(i):
             nc.scalar.copy(
-                out=a_grouped[:, i, :, :]
-                .rearrange("p n j -> p (n j)")
-                .bitcast(F32)
-                .rearrange("p (n u) -> p n u", u=2),
+                out=words(a_grouped[:, i, :, :], "p (n u) -> p n u", u=2),
                 in_=a_banks[i][:].rearrange("p u n -> p n u"),
             )
 
-        for i in range(TILES + 1):
-            if i < TILES:
-                normalise_and_transpose(i)
-            if i > 0:
-                group_nadj(i - 1)
+        def quantise_nadj(i):
+            nc.vector.quantize_mx(
+                out=a_codes[:, i * P : (i + 1) * P].bitcast(FP8X4),
+                scales=a_scales[:, i * P : (i + 1) * P],
+                in_=a_grouped[:, i, :, :].rearrange("p n j -> p (n j)"),
+            )
 
         w_grouped = keep.tile([P, TILES, P, PACK], BF16, align_bytes=64)
         w_codes = keep.tile([P, FEATS], U32, align_bytes=64)
         w_scales = keep.tile([P, FEATS], U8, align_bytes=64)
-        w_banks = []
-        for i in range(TILES):
-            w_bank = psum.tile([P, 2, P], F32, tag="bank", name="w_bank")
+        w_banks = {}
+
+        def transpose_wt(i):
+            w_bank = aux_psum.tile([P, 2, P], F32, tag="aux", name="w_bank")
             wt_words = wt_sb[:, i, :].bitcast(F32)
             for u in range(2):
                 nc.tensor.transpose(
                     out=w_bank[:, u, :], in_=wt_words[:, u * P : (u + 1) * P], identity=ident_f32[:]
                 )
-            w_banks.append(w_bank)
+            w_banks[i] = w_bank
+
+        def group_wt(i, engine_copy):
+            engine_copy(
+                out=words(w_grouped[:, i, :, :], "p (o u) -> p o u", u=2),
+                in_=w_banks[i][:].rearrange("p u o -> p o u"),
+            )
+
+        def quantise_wt():
+            nc.vector.quantize_mx(
+                out=w_codes[:].bitcast(FP8X4),
+                scales=w_scales[:],
+                in_=w_grouped[:].rearrange("p i o j -> p (i o j)"),
+            )
 
         q_grouped = keep.tile([P, GRAPHS, FEATS, PACK], BF16, align_bytes=64)
         q_codes = keep.tile([P, GRAPHS, FEATS], U32, align_bytes=64)
         q_scales = keep.tile([P, GRAPHS, FEATS], U8, align_bytes=64)
+        i_banks = {}
 
         def group_query(g):
             nc.vector.tensor_copy(
                 out=q_grouped[:, g, :, :].rearrange("p (e c) j -> p e c j", e=2),
                 in_=query_sb[:, g, :, :].rearrange("p j (c e) -> p e c j", e=2),
+            )
+
+        def interleave_on_tensor(g, e):
+            i_bank = aux_psum.tile([P, 2, P * PACK], BF16, tag="aux", name="i_bank")
+            for u in range(2):
+                nc.tensor.matmul(
+                    out=i_bank[:, u, :].rearrange("p (q j) -> p q j", j=PACK),
+                    lhsT=ident[:],
+                    rhs=query_sb[:, g, :, 2 * P * u + e : 2 * P * (u + 1) : 2].rearrange(
+                        "p j q -> p q j"
+                    ),
+                    start=True,
+                    stop=True,
+                )
+            i_banks[(g, e)] = i_bank
+
+        def fetch_interleaved(g, e):
+            nc.scalar.copy(
+                out=words(q_grouped[:, g, 2 * P * e : 2 * P * (e + 1), :], "p w -> p w"),
+                in_=words(i_banks[(g, e)][:], "p w -> p w"),
             )
 
         def quantise_query(g):
@@ -139,59 +181,11 @@ def tile_gatedspatialattentionlayer_pc_kernel(tc, adj, query, Wt, bt, out):
                 in_=q_grouped[:, g, :, :].rearrange("p d j -> p (d j)"),
             )
 
-        i_banks = {}
-
-        def interleave_on_tensor(g):
-            for e in range(2):
-                i_bank = psum.tile([P, 2, P * PACK], BF16, tag="bank", name="i_bank")
-                for u in range(2):
-                    nc.tensor.matmul(
-                        out=i_bank[:, u, :].rearrange("p (q j) -> p q j", j=PACK),
-                        lhsT=ident[:],
-                        rhs=query_sb[:, g, :, 2 * P * u + e : 2 * P * (u + 1) : 2].rearrange(
-                            "p j q -> p q j"
-                        ),
-                        start=True,
-                        stop=True,
-                    )
-                i_banks[(g, e)] = i_bank
-
-        def fetch_interleaved(g, e):
-            nc.scalar.copy(
-                out=q_grouped[:, g, 2 * P * e : 2 * P * (e + 1), :]
-                .rearrange("p c j -> p (c j)")
-                .bitcast(F32),
-                in_=i_banks[(g, e)][:].rearrange("p u c -> p (u c)").bitcast(F32),
-            )
-
-        group_query(0)
-        interleave_on_tensor(1)
-        quantise_query(0)
-        nc.vector.quantize_mx(
-            out=a_codes[:].bitcast(FP8X4),
-            scales=a_scales[:],
-            in_=a_grouped[:].rearrange("p i n j -> p (i n j)"),
-        )
-        for i in range(TILES):
-            nc.scalar.copy(
-                out=w_grouped[:, i, :, :]
-                .rearrange("p o j -> p (o j)")
-                .bitcast(F32)
-                .rearrange("p (o u) -> p o u", u=2),
-                in_=w_banks[i][:].rearrange("p u o -> p o u"),
-            )
-        fetch_interleaved(1, 0)
-        nc.vector.quantize_mx(
-            out=w_codes[:].bitcast(FP8X4),
-            scales=w_scales[:],
-            in_=w_grouped[:].rearrange("p i o j -> p (i o j)"),
-        )
-
-        gq_banks, gq_groupeds, out_banks, biaseds = {}, {}, {}, {}
+        gq_banks, gq_groupeds, out_banks = {}, {}, {}
 
         def first_product(u):
             g, cols = u // TILES, slice((u % TILES) * P, (u % TILES + 1) * P)
-            gq_bank = psum.tile([P, PACK, P], F32, tag="bank", name="gq_bank")
+            gq_bank = gq_psum.tile([P, PACK, P], F32, tag="gq", name="gq_bank")
             for j in range(PACK):
                 block = slice((2 * (j % 2) + j // 2) * P, (2 * (j % 2) + j // 2 + 1) * P)
                 nc.tensor.matmul_mx(
@@ -218,7 +212,7 @@ def tile_gatedspatialattentionlayer_pc_kernel(tc, adj, query, Wt, bt, out):
                 scales=gq_scales[:],
                 in_=gq_groupeds[u][:].rearrange("p n j -> p (n j)"),
             )
-            out_bank = psum.tile([P, FEATS], F32, tag="bank", name="out_bank")
+            out_bank = out_psum.tile([P, FEATS], F32, tag="out", name="out_bank")
             nc.tensor.matmul_mx(
                 out=out_bank[:],
                 lhsT=gq_codes[:].bitcast(FP8X4),
@@ -230,37 +224,83 @@ def tile_gatedspatialattentionlayer_pc_kernel(tc, adj, query, Wt, bt, out):
             )
             out_banks[u] = out_bank
 
-        def add_bias(u):
+        def finish(u):
             biased = work.tile([P, FEATS], F32, tag="biased")
             nc.vector.tensor_tensor(out=biased[:], in0=out_banks[u][:], in1=bias_sb[:], op=ALU.add)
-            biaseds[u] = biased
-
-        def relu_and_store(u):
             result = work.tile([P, FEATS], F32, tag="result")
-            if u % 2 == 1:
-                nc.vector.tensor_scalar_max(out=result[:], in0=biaseds[u][:], scalar1=0.0)
+            if u == UNITS - 1:
+                nc.vector.tensor_scalar_max(out=result[:], in0=biased[:], scalar1=0.0)
+            elif u >= UNITS - 3:
+                nc.scalar.activation(out=result[:], in_=biased[:], func=ACT.Relu)
             else:
-                nc.scalar.activation(out=result[:], in_=biaseds[u][:], func=ACT.Relu)
+                nc.gpsimd.tensor_scalar(
+                    out=result[:], in0=biased[:], scalar1=FLT_MAX, scalar2=0.0, op0=ALU.min, op1=ALU.max
+                )
             nc.sync.dma_start(out=out_rows[u * P : (u + 1) * P, :], in_=result[:])
 
+        sum_row(0)
+        sum_row(1)
+        add_self_loops(0)
+        add_self_loops(1)
+        add_self_loops(2)
+        normalise(0)
+        transpose_nadj(0)
+        add_self_loops(3)
+        sum_row(2)
+        normalise(1)
+        transpose_nadj(1)
+        group_nadj(0)
+        sum_row(3)
+        group_nadj(1)
+        group_query(0)
+        normalise(2)
+        transpose_wt(0)
+        transpose_nadj(2)
+        quantise_nadj(0)
+        quantise_query(0)
+        transpose_wt(1)
+        transpose_wt(2)
         first_product(0)
-        for step in range(UNITS + RELU_LAG):
+        transpose_wt(3)
+        quantise_nadj(1)
+        first_product(1)
+        normalise(3)
+        transpose_nadj(3)
+        group_nadj(2)
+        group_wt(0, nc.scalar.copy)
+        group_wt(1, nc.scalar.copy)
+        quantise_nadj(2)
+        group_wt(2, nc.vector.tensor_copy)
+        group_wt(3, nc.vector.tensor_copy)
+        round_gq(0)
+        group_nadj(3)
+        quantise_wt()
+        quantise_nadj(3)
+        interleave_on_tensor(1, 0)
+        interleave_on_tensor(1, 1)
+
+        for step in range(UNITS + 2):
             g, i = step // TILES, step % TILES
-            if step + 1 < UNITS:
+            if 0 <= step - 1 < UNITS:
+                second_product(step - 1)
+            if 1 <= step and step + 1 < UNITS:
                 first_product(step + 1)
             if i == 2 and g + 2 < GRAPHS:
-                interleave_on_tensor(g + 2)
-            if step < UNITS:
+                interleave_on_tensor(g + 2, 0)
+            if i == 3 and g + 2 < GRAPHS:
+                interleave_on_tensor(g + 2, 1)
+            if 1 <= step < UNITS:
                 round_gq(step)
-            if i == 0 and g + 1 < GRAPHS:
-                fetch_interleaved(g + 1, 1)
+            if step == 1:
+                fetch_interleaved(1, 0)
+                fetch_interleaved(1, 1)
             if i == 3 and g + 2 < GRAPHS:
                 fetch_interleaved(g + 2, 0)
-            if 0 <= step - QUANTISE_LAG < UNITS:
-                second_product(step - QUANTISE_LAG)
-            if 0 <= step - BIAS_LAG < UNITS:
-                add_bias(step - BIAS_LAG)
-            if i == 1 and g + 1 < GRAPHS:
+            if i == 0 and 1 <= g and g + 1 < GRAPHS:
+                fetch_interleaved(g + 1, 1)
+            if 0 <= step - 2 < UNITS:
+                finish(step - 2)
+            if step == 2:
+                quantise_query(1)
+            if i == 1 and 1 <= g and g + 1 < GRAPHS:
                 quantise_query(g + 1)
-            if 0 <= step - RELU_LAG < UNITS:
-                relu_and_store(step - RELU_LAG)

@@ -32,9 +32,8 @@ def tile_gatedspatialattentionlayer_pc_kernel(tc, adj, query, Wt, bt, out):
 
     with tc.tile_pool(name="keep", bufs=1) as keep, tc.tile_pool(
         name="work", bufs=6
-    ) as work, tc.psum_pool(name="gq_psum", bufs=2) as gq_psum, tc.psum_pool(
-        name="out_psum", bufs=2
-    ) as out_psum, tc.psum_pool(name="aux_psum", bufs=4) as aux_psum, tc.manual_schedule():
+    ) as work, tc.psum_pool(name="psum", bufs=8) as psum, tc.manual_schedule():
+
         adj_sb = keep.tile([P, TILES, NODES], BF16)
         query_sb = keep.tile([P, GRAPHS, PACK, FEATS], BF16)
         wt_sb = keep.tile([P, TILES, FEATS], BF16)
@@ -53,12 +52,10 @@ def tile_gatedspatialattentionlayer_pc_kernel(tc, adj, query, Wt, bt, out):
         load_query(0)
         nc.sync.dma_start(out=wt_sb[:], in_=Wt.rearrange("(i p) d -> p i d", p=P))
         load_query(1)
-        nc.sync.dma_start(out=bias_sb[:], in_=bt.partition_broadcast(P))
         load_query(2)
         load_query(3)
+        nc.sync.dma_start(out=bias_sb[:], in_=bt.partition_broadcast(P))
 
-        ident = keep.tile([P, P], BF16)
-        make_identity(nc, ident[:])
         ident_f32 = keep.tile([P, P], F32)
         make_identity(nc, ident_f32[:])
 
@@ -95,7 +92,7 @@ def tile_gatedspatialattentionlayer_pc_kernel(tc, adj, query, Wt, bt, out):
             nadjs[i] = nadj
 
         def transpose_nadj(i):
-            a_bank = aux_psum.tile([P, 2, P], F32, tag="aux", name="a_bank")
+            a_bank = psum.tile([P, 2, P], F32, tag="bank", name="a_bank")
             nadj_words = nadjs[i][:].bitcast(F32)
             for u in range(2):
                 nc.tensor.transpose(
@@ -122,7 +119,7 @@ def tile_gatedspatialattentionlayer_pc_kernel(tc, adj, query, Wt, bt, out):
         w_banks = {}
 
         def transpose_wt(i):
-            w_bank = aux_psum.tile([P, 2, P], F32, tag="aux", name="w_bank")
+            w_bank = psum.tile([P, 2, P], F32, tag="bank", name="w_bank")
             wt_words = wt_sb[:, i, :].bitcast(F32)
             for u in range(2):
                 nc.tensor.transpose(
@@ -146,7 +143,6 @@ def tile_gatedspatialattentionlayer_pc_kernel(tc, adj, query, Wt, bt, out):
         q_grouped = keep.tile([P, GRAPHS, FEATS, PACK], BF16, align_bytes=64)
         q_codes = keep.tile([P, GRAPHS, FEATS], U32, align_bytes=64)
         q_scales = keep.tile([P, GRAPHS, FEATS], U8, align_bytes=64)
-        i_banks = {}
 
         def group_query(g):
             nc.vector.tensor_copy(
@@ -154,24 +150,11 @@ def tile_gatedspatialattentionlayer_pc_kernel(tc, adj, query, Wt, bt, out):
                 in_=query_sb[:, g, :, :].rearrange("p j (c e) -> p e c j", e=2),
             )
 
-        def interleave_on_tensor(g, e):
-            i_bank = aux_psum.tile([P, 2, P * PACK], BF16, tag="aux", name="i_bank")
-            for u in range(2):
-                nc.tensor.matmul(
-                    out=i_bank[:, u, :].rearrange("p (q j) -> p q j", j=PACK),
-                    lhsT=ident[:],
-                    rhs=query_sb[:, g, :, 2 * P * u + e : 2 * P * (u + 1) : 2].rearrange(
-                        "p j q -> p q j"
-                    ),
-                    start=True,
-                    stop=True,
-                )
-            i_banks[(g, e)] = i_bank
-
-        def fetch_interleaved(g, e):
+        def group_query_on_scalar(g, k):
+            e, first = k // 2, 2 * P * (k % 2)
             nc.scalar.copy(
-                out=words(q_grouped[:, g, 2 * P * e : 2 * P * (e + 1), :], "p w -> p w"),
-                in_=words(i_banks[(g, e)][:], "p w -> p w"),
+                out=q_grouped[:, g, k * P : (k + 1) * P, :],
+                in_=query_sb[:, g, :, first + e : first + 2 * P : 2].rearrange("p j c -> p c j"),
             )
 
         def quantise_query(g):
@@ -185,7 +168,7 @@ def tile_gatedspatialattentionlayer_pc_kernel(tc, adj, query, Wt, bt, out):
 
         def first_product(u):
             g, cols = u // TILES, slice((u % TILES) * P, (u % TILES + 1) * P)
-            gq_bank = gq_psum.tile([P, PACK, P], F32, tag="gq", name="gq_bank")
+            gq_bank = psum.tile([P, PACK, P], F32, tag="bank", name="gq_bank")
             for j in range(PACK):
                 block = slice((2 * (j % 2) + j // 2) * P, (2 * (j % 2) + j // 2 + 1) * P)
                 nc.tensor.matmul_mx(
@@ -212,7 +195,7 @@ def tile_gatedspatialattentionlayer_pc_kernel(tc, adj, query, Wt, bt, out):
                 scales=gq_scales[:],
                 in_=gq_groupeds[u][:].rearrange("p n j -> p (n j)"),
             )
-            out_bank = out_psum.tile([P, FEATS], F32, tag="out", name="out_bank")
+            out_bank = psum.tile([P, FEATS], F32, tag="bank", name="out_bank")
             nc.tensor.matmul_mx(
                 out=out_bank[:],
                 lhsT=gq_codes[:].bitcast(FP8X4),
@@ -230,8 +213,6 @@ def tile_gatedspatialattentionlayer_pc_kernel(tc, adj, query, Wt, bt, out):
             result = work.tile([P, FEATS], F32, tag="result")
             if u == UNITS - 1:
                 nc.vector.tensor_scalar_max(out=result[:], in0=biased[:], scalar1=0.0)
-            elif u >= UNITS - 3:
-                nc.scalar.activation(out=result[:], in_=biased[:], func=ACT.Relu)
             else:
                 nc.gpsimd.tensor_scalar(
                     out=result[:], in0=biased[:], scalar1=FLT_MAX, scalar2=0.0, op0=ALU.min, op1=ALU.max
@@ -253,54 +234,47 @@ def tile_gatedspatialattentionlayer_pc_kernel(tc, adj, query, Wt, bt, out):
         sum_row(3)
         group_nadj(1)
         group_query(0)
-        normalise(2)
         transpose_wt(0)
-        transpose_nadj(2)
-        quantise_nadj(0)
-        quantise_query(0)
         transpose_wt(1)
+        normalise(2)
+        transpose_nadj(2)
         transpose_wt(2)
-        first_product(0)
         transpose_wt(3)
-        quantise_nadj(1)
-        first_product(1)
-        normalise(3)
-        transpose_nadj(3)
-        group_nadj(2)
         group_wt(0, nc.scalar.copy)
         group_wt(1, nc.scalar.copy)
-        quantise_nadj(2)
-        group_wt(2, nc.vector.tensor_copy)
-        group_wt(3, nc.vector.tensor_copy)
+        quantise_nadj(0)
+        quantise_query(0)
+        first_product(0)
+        group_nadj(2)
+        group_wt(2, nc.scalar.copy)
+        normalise(3)
+        transpose_nadj(3)
+        quantise_nadj(1)
+        first_product(1)
         round_gq(0)
+        group_wt(3, nc.scalar.copy)
         group_nadj(3)
-        quantise_wt()
+        group_query(1)
+        round_gq(1)
+        quantise_nadj(2)
+        first_product(2)
         quantise_nadj(3)
-        interleave_on_tensor(1, 0)
-        interleave_on_tensor(1, 1)
+        first_product(3)
+        quantise_query(1)
+        quantise_wt()
 
-        for step in range(UNITS + 2):
-            g, i = step // TILES, step % TILES
-            if 0 <= step - 1 < UNITS:
-                second_product(step - 1)
-            if 1 <= step and step + 1 < UNITS:
+        for step in range(UNITS + 3):
+            if 4 <= step + 1 < UNITS:
                 first_product(step + 1)
-            if i == 2 and g + 2 < GRAPHS:
-                interleave_on_tensor(g + 2, 0)
-            if i == 3 and g + 2 < GRAPHS:
-                interleave_on_tensor(g + 2, 1)
-            if 1 <= step < UNITS:
+            if 2 <= step < UNITS:
                 round_gq(step)
-            if step == 1:
-                fetch_interleaved(1, 0)
-                fetch_interleaved(1, 1)
-            if i == 3 and g + 2 < GRAPHS:
-                fetch_interleaved(g + 2, 0)
-            if i == 0 and 1 <= g and g + 1 < GRAPHS:
-                fetch_interleaved(g + 1, 1)
+            if 1 <= step <= 8:
+                group_query_on_scalar(2 + (step - 1) // 4, (step - 1) % 4)
             if 0 <= step - 2 < UNITS:
-                finish(step - 2)
-            if step == 2:
-                quantise_query(1)
-            if i == 1 and 1 <= g and g + 1 < GRAPHS:
-                quantise_query(g + 1)
+                second_product(step - 2)
+            if 0 <= step - 3 < UNITS:
+                finish(step - 3)
+            if step == 5:
+                quantise_query(2)
+            if step == 10:
+                quantise_query(3)

@@ -17,6 +17,7 @@ GRAPHS = 4
 TILES = NODES // P
 UNITS = GRAPHS * TILES
 FLT_MAX = 3.4028234663852886e38
+FIRST_SCALAR_RELU = 11
 
 FLOPS = 2 * 2 * GRAPHS * NODES * NODES * FEATS
 
@@ -82,8 +83,10 @@ def tile_gatedspatialattentionlayer_pc_kernel(tc, adj, query, Wt, bt, out):
                 out=a_diag[:, i, :], in0=adj_sb[:, i, i * P : (i + 1) * P], in1=ident_f32[:], op=ALU.add
             )
 
-        def normalise(i):
+        def invert_sum(i):
             nc.vector.reciprocal(out=inv_sum[:, i : i + 1], in_=row_sum[:, i : i + 1])
+
+        def normalise(i):
             nadj = work.tile([P, NODES], BF16, tag="nadj")
             nc.vector.tensor_scalar_mul(out=nadj[:], in0=adj_sb[:, i, :], scalar1=inv_sum[:, i : i + 1])
             nc.vector.tensor_scalar_mul(
@@ -164,7 +167,7 @@ def tile_gatedspatialattentionlayer_pc_kernel(tc, adj, query, Wt, bt, out):
                 in_=q_grouped[:, g, :, :].rearrange("p d j -> p (d j)"),
             )
 
-        gq_banks, gq_groupeds, out_banks = {}, {}, {}
+        gq_banks, gq_groupeds, out_banks, biaseds = {}, {}, {}, {}
 
         def first_product(u):
             g, cols = u // TILES, slice((u % TILES) * P, (u % TILES + 1) * P)
@@ -207,12 +210,18 @@ def tile_gatedspatialattentionlayer_pc_kernel(tc, adj, query, Wt, bt, out):
             )
             out_banks[u] = out_bank
 
-        def finish(u):
+        def add_bias(u):
             biased = work.tile([P, FEATS], F32, tag="biased")
             nc.vector.tensor_tensor(out=biased[:], in0=out_banks[u][:], in1=bias_sb[:], op=ALU.add)
+            biaseds[u] = biased
+
+        def relu_and_store(u):
+            biased = biaseds[u]
             result = work.tile([P, FEATS], F32, tag="result")
             if u == UNITS - 1:
                 nc.vector.tensor_scalar_max(out=result[:], in0=biased[:], scalar1=0.0)
+            elif u >= FIRST_SCALAR_RELU:
+                nc.scalar.activation(out=result[:], in_=biased[:], func=ACT.Relu)
             else:
                 nc.gpsimd.tensor_scalar(
                     out=result[:], in0=biased[:], scalar1=FLT_MAX, scalar2=0.0, op0=ALU.min, op1=ALU.max
@@ -224,18 +233,22 @@ def tile_gatedspatialattentionlayer_pc_kernel(tc, adj, query, Wt, bt, out):
         add_self_loops(0)
         add_self_loops(1)
         add_self_loops(2)
+        invert_sum(0)
+        add_self_loops(3)
         normalise(0)
         transpose_nadj(0)
-        add_self_loops(3)
         sum_row(2)
-        normalise(1)
-        transpose_nadj(1)
+        invert_sum(1)
         group_nadj(0)
         sum_row(3)
+        normalise(1)
+        transpose_nadj(1)
+        invert_sum(2)
         group_nadj(1)
         group_query(0)
         transpose_wt(0)
         transpose_wt(1)
+        invert_sum(3)
         normalise(2)
         transpose_nadj(2)
         transpose_wt(2)
@@ -272,8 +285,13 @@ def tile_gatedspatialattentionlayer_pc_kernel(tc, adj, query, Wt, bt, out):
                 group_query_on_scalar(2 + (step - 1) // 4, (step - 1) % 4)
             if 0 <= step - 2 < UNITS:
                 second_product(step - 2)
+            if step == UNITS - 1:
+                for u in range(FIRST_SCALAR_RELU, step - 3):
+                    relu_and_store(u)
             if 0 <= step - 3 < UNITS:
-                finish(step - 3)
+                add_bias(step - 3)
+                if step - 3 < FIRST_SCALAR_RELU or step >= UNITS - 1:
+                    relu_and_store(step - 3)
             if step == 5:
                 quantise_query(2)
             if step == 10:

@@ -153,6 +153,12 @@ def tile_gatedspatialattentionlayer_pc_kernel(tc, adj, query, Wt, bt, out):
                 in_=query_sb[:, g, :, :].rearrange("p j (c e) -> p e c j", e=2),
             )
 
+        def group_half_query(g, e):
+            nc.vector.tensor_copy(
+                out=q_grouped[:, g, 2 * P * e : 2 * P * (e + 1), :],
+                in_=query_sb[:, g, :, e : FEATS : 2].rearrange("p j c -> p c j"),
+            )
+
         def group_query_on_scalar(g, k):
             e, first = k // 2, 2 * P * (k % 2)
             nc.scalar.copy(
@@ -281,8 +287,10 @@ def tile_gatedspatialattentionlayer_pc_kernel(tc, adj, query, Wt, bt, out):
                 first_product(step + 1)
             if 2 <= step < UNITS:
                 round_gq(step)
-            if 1 <= step <= 8:
-                group_query_on_scalar(2 + (step - 1) // 4, (step - 1) % 4)
+            if 1 <= step <= 2:
+                group_query_on_scalar(2, step - 1)
+            if 4 <= step <= 7:
+                group_query_on_scalar(3, step - 4)
             if 0 <= step - 2 < UNITS:
                 second_product(step - 2)
             if step == UNITS - 1:
@@ -292,6 +300,8 @@ def tile_gatedspatialattentionlayer_pc_kernel(tc, adj, query, Wt, bt, out):
                 add_bias(step - 3)
                 if step - 3 < FIRST_SCALAR_RELU or step >= UNITS - 1:
                     relu_and_store(step - 3)
+            if step == 2:
+                group_half_query(2, 1)
             if step == 5:
                 quantise_query(2)
             if step == 10:

@@ -149,8 +149,8 @@ def tile_gatedspatialattentionlayer_pc_kernel(tc, adj, query, Wt, bt, out):
 
         def group_query(g):
             nc.vector.tensor_copy(
-                out=q_grouped[:, g, :, :].rearrange("p (e c) j -> p e c j", e=2),
-                in_=query_sb[:, g, :, :].rearrange("p j (c e) -> p e c j", e=2),
+                out=q_grouped[:, g, :, :].rearrange("p (e c) j -> p c e j", e=2),
+                in_=query_sb[:, g, :, :].rearrange("p j (c e) -> p c e j", e=2),
             )
 
         def group_half_query(g, e):

@@ -153,18 +153,21 @@ def tile_gatedspatialattentionlayer_pc_kernel(tc, adj, query, Wt, bt, out):
                 in_=query_sb[:, g, :, :].rearrange("p j (c e) -> p c e j", e=2),
             )
 
-        def group_half_query(g, e):
-            nc.vector.tensor_copy(
-                out=q_grouped[:, g, 2 * P * e : 2 * P * (e + 1), :],
-                in_=query_sb[:, g, :, e : FEATS : 2].rearrange("p j c -> p c j"),
+        def group_part_of_query(engine_copy, g, first, count):
+            engine_copy(
+                out=q_grouped[:, g, :, :].rearrange("p (e c) j -> p c e j", e=2)[
+                    :, first : first + count, :, :
+                ],
+                in_=query_sb[:, g, :, :].rearrange("p j (c e) -> p c e j", e=2)[
+                    :, first : first + count, :, :
+                ],
             )
 
+        def group_half_query(g):
+            group_part_of_query(nc.vector.tensor_copy, g, P, P)
+
         def group_query_on_scalar(g, k):
-            e, first = k // 2, 2 * P * (k % 2)
-            nc.scalar.copy(
-                out=q_grouped[:, g, k * P : (k + 1) * P, :],
-                in_=query_sb[:, g, :, first + e : first + 2 * P : 2].rearrange("p j c -> p c j"),
-            )
+            group_part_of_query(nc.scalar.copy, g, k * (P // 2), P // 2)
 
         def quantise_query(g):
             nc.vector.quantize_mx(
@@ -301,7 +304,7 @@ def tile_gatedspatialattentionlayer_pc_kernel(tc, adj, query, Wt, bt, out):
                 if step - 3 < FIRST_SCALAR_RELU or step >= UNITS - 1:
                     relu_and_store(step - 3)
             if step == 2:
-                group_half_query(2, 1)
+                group_half_query(2)
             if step == 5:
                 quantise_query(2)
             if step == 10:

@@ -148,19 +148,13 @@ def tile_gatedspatialattentionlayer_pc_kernel(tc, adj, query, Wt, bt, out):
         q_scales = keep.tile([P, GRAPHS, FEATS], U8, align_bytes=64)
 
         def group_query(g):
-            nc.vector.tensor_copy(
-                out=q_grouped[:, g, :, :].rearrange("p (e c) j -> p c e j", e=2),
-                in_=query_sb[:, g, :, :].rearrange("p j (c e) -> p c e j", e=2),
-            )
+            group_part_of_query(nc.vector.tensor_copy, g, 0, 2 * P)
 
         def group_part_of_query(engine_copy, g, first, count):
+            part = slice(first // 2, (first + count) // 2)
             engine_copy(
-                out=q_grouped[:, g, :, :].rearrange("p (e c) j -> p c e j", e=2)[
-                    :, first : first + count, :, :
-                ],
-                in_=query_sb[:, g, :, :].rearrange("p j (c e) -> p c e j", e=2)[
-                    :, first : first + count, :, :
-                ],
+                out=q_grouped[:, g, :, :].rearrange("p (e q r) j -> p q j e r", e=2, r=2)[:, part],
+                in_=query_sb[:, g, :, :].rearrange("p j (q r e) -> p q j e r", r=2, e=2)[:, part],
             )
 
         def group_half_query(g):

@@ -17,7 +17,8 @@ GRAPHS = 4
 TILES = NODES // P
 UNITS = GRAPHS * TILES
 FLT_MAX = 3.4028234663852886e38
-FIRST_SCALAR_RELU = 11
+GPSIMD_COLS = 384
+FIRST_SHARED_RELU = 4
 
 FLOPS = 2 * 2 * GRAPHS * NODES * NODES * FEATS
 
@@ -223,12 +224,19 @@ def tile_gatedspatialattentionlayer_pc_kernel(tc, adj, query, Wt, bt, out):
             result = work.tile([P, FEATS], F32, tag="result")
             if u == UNITS - 1:
                 nc.vector.tensor_scalar_max(out=result[:], in0=biased[:], scalar1=0.0)
-            elif u >= FIRST_SCALAR_RELU:
-                nc.scalar.activation(out=result[:], in_=biased[:], func=ACT.Relu)
             else:
-                nc.gpsimd.tensor_scalar(
-                    out=result[:], in0=biased[:], scalar1=FLT_MAX, scalar2=0.0, op0=ALU.min, op1=ALU.max
-                )
+                cols = FEATS if u < FIRST_SHARED_RELU else 0 if u == UNITS - 2 else GPSIMD_COLS
+                if cols > 0:
+                    nc.gpsimd.tensor_scalar(
+                        out=result[:, :cols],
+                        in0=biased[:, :cols],
+                        scalar1=FLT_MAX,
+                        scalar2=0.0,
+                        op0=ALU.min,
+                        op1=ALU.max,
+                    )
+                if cols < FEATS:
+                    nc.scalar.activation(out=result[:, cols:], in_=biased[:, cols:], func=ACT.Relu)
             nc.sync.dma_start(out=out_rows[u * P : (u + 1) * P, :], in_=result[:])
 
         sum_row(0)
@@ -290,13 +298,12 @@ def tile_gatedspatialattentionlayer_pc_kernel(tc, adj, query, Wt, bt, out):
                 group_query_on_scalar(3, step - 4)
             if 0 <= step - 2 < UNITS:
                 second_product(step - 2)
-            if step == UNITS - 1:
-                for u in range(FIRST_SCALAR_RELU, step - 3):
-                    relu_and_store(u)
             if 0 <= step - 3 < UNITS:
                 add_bias(step - 3)
-                if step - 3 < FIRST_SCALAR_RELU or step >= UNITS - 1:
-                    relu_and_store(step - 3)
+            if FIRST_SHARED_RELU <= step - 4 < UNITS - 1:
+                relu_and_store(step - 4)
+            if 0 <= step - 3 < FIRST_SHARED_RELU or step - 3 == UNITS - 1:
+                relu_and_store(step - 3)
             if step == 2:
                 group_half_query(2)
             if step == 5:

@@ -33,7 +33,7 @@ def tile_gatedspatialattentionlayer_pc_kernel(tc, adj, query, Wt, bt, out):
     out_rows = out.flatten_outer_dims()
 
     with tc.tile_pool(name="keep", bufs=1) as keep, tc.tile_pool(
-        name="work", bufs=6
+        name="work", bufs=UNITS
     ) as work, tc.psum_pool(name="psum", bufs=8) as psum, tc.manual_schedule():
 
         adj_sb = keep.tile([P, TILES, NODES], BF16)

@@ -88,12 +88,13 @@ def tile_gatedspatialattentionlayer_pc_kernel(tc, adj, query, Wt, bt, out):
             nc.vector.reciprocal(out=inv_sum[:, i : i + 1], in_=row_sum[:, i : i + 1])
 
         def normalise(i):
-            nadj = work.tile([P, NODES], BF16, tag="nadj")
-            nc.vector.tensor_scalar_mul(out=nadj[:], in0=adj_sb[:, i, :], scalar1=inv_sum[:, i : i + 1])
+            nadjs[i] = work.tile([P, NODES], BF16, tag="nadj", name="nadj")
+            nc.vector.tensor_scalar_mul(out=nadjs[i][:], in0=adj_sb[:, i, :], scalar1=inv_sum[:, i : i + 1])
+
+        def normalise_diagonal(i):
             nc.vector.tensor_scalar_mul(
-                out=nadj[:, i * P : (i + 1) * P], in0=a_diag[:, i, :], scalar1=inv_sum[:, i : i + 1]
+                out=nadjs[i][:, i * P : (i + 1) * P], in0=a_diag[:, i, :], scalar1=inv_sum[:, i : i + 1]
             )
-            nadjs[i] = nadj
 
         def transpose_nadj(i):
             a_bank = psum.tile([P, 2, P], F32, tag="bank", name="a_bank")
@@ -223,7 +224,9 @@ def tile_gatedspatialattentionlayer_pc_kernel(tc, adj, query, Wt, bt, out):
             biased = biaseds[u]
             result = work.tile([P, FEATS], F32, tag="result")
             if u == UNITS - 1:
-                nc.vector.tensor_scalar_max(out=result[:], in0=biased[:], scalar1=0.0)
+                half = slice(0, FEATS // 2), slice(FEATS // 2, FEATS)
+                nc.vector.tensor_scalar_max(out=result[:, half[0]], in0=biased[:, half[0]], scalar1=0.0)
+                nc.scalar.activation(out=result[:, half[1]], in_=biased[:, half[1]], func=ACT.Relu)
             else:
                 cols = FEATS if u < FIRST_SHARED_RELU else 0 if u == UNITS - 2 else GPSIMD_COLS
                 if cols > 0:
@@ -243,38 +246,42 @@ def tile_gatedspatialattentionlayer_pc_kernel(tc, adj, query, Wt, bt, out):
         sum_row(1)
         add_self_loops(0)
         add_self_loops(1)
-        add_self_loops(2)
         invert_sum(0)
-        add_self_loops(3)
         normalise(0)
-        transpose_nadj(0)
+        add_self_loops(2)
         sum_row(2)
+        add_self_loops(3)
         invert_sum(1)
-        group_nadj(0)
+        normalise_diagonal(0)
+        transpose_nadj(0)
         sum_row(3)
-        normalise(1)
-        transpose_nadj(1)
         invert_sum(2)
-        group_nadj(1)
+        normalise(1)
+        group_nadj(0)
+        normalise(2)
+        normalise_diagonal(1)
+        transpose_nadj(1)
         group_query(0)
+        group_nadj(1)
+        invert_sum(3)
         transpose_wt(0)
         transpose_wt(1)
-        invert_sum(3)
-        normalise(2)
+        quantise_nadj(0)
+        normalise_diagonal(2)
         transpose_nadj(2)
         transpose_wt(2)
         transpose_wt(3)
+        normalise(3)
         group_wt(0, nc.scalar.copy)
         group_wt(1, nc.scalar.copy)
-        quantise_nadj(0)
         quantise_query(0)
         first_product(0)
-        group_nadj(2)
-        group_wt(2, nc.scalar.copy)
-        normalise(3)
-        transpose_nadj(3)
         quantise_nadj(1)
         first_product(1)
+        group_nadj(2)
+        group_wt(2, nc.scalar.copy)
+        normalise_diagonal(3)
+        transpose_nadj(3)
         round_gq(0)
         group_wt(3, nc.scalar.copy)
         group_nadj(3)
@@ -282,10 +289,10 @@ def tile_gatedspatialattentionlayer_pc_kernel(tc, adj, query, Wt, bt, out):
         round_gq(1)
         quantise_nadj(2)
         first_product(2)
+        quantise_wt()
+        quantise_query(1)
         quantise_nadj(3)
         first_product(3)
-        quantise_query(1)
-        quantise_wt()
 
         for step in range(UNITS + 3):
             if 4 <= step + 1 < UNITS:
@@ -308,5 +315,5 @@ def tile_gatedspatialattentionlayer_pc_kernel(tc, adj, query, Wt, bt, out):
                 group_half_query(2)
             if step == 5:
                 quantise_query(2)
-            if step == 10:
+            if step == 9:
                 quantise_query(3)

@@ -39,7 +39,11 @@ def tile_gatedspatialattentionlayer_pc_kernel(tc, adj, query, Wt, bt, out):
         adj_sb = keep.tile([P, TILES, NODES], BF16)
         query_sb = keep.tile([P, GRAPHS, PACK, FEATS], BF16)
         wt_sb = keep.tile([P, TILES, FEATS], BF16)
+        bias_rows = keep.tile([P, FEATS], BF16)
         bias_sb = keep.tile([P, FEATS], BF16)
+        ones = keep.tile([P, P], BF16)
+        nc.vector.memset(bias_rows[:], 0.0)
+        nc.vector.memset(ones[:], 1.0)
 
         def load_query(g):
             nc.sync.dma_start(
@@ -52,11 +56,11 @@ def tile_gatedspatialattentionlayer_pc_kernel(tc, adj, query, Wt, bt, out):
         for i in range(TILES):
             nc.sync.dma_start(out=adj_sb[:, i, :], in_=adj[i * P : (i + 1) * P, :])
         load_query(0)
+        nc.sync.dma_start(out=bias_rows[:1, :], in_=bt.rearrange("(a d) -> a d", a=1))
         nc.sync.dma_start(out=wt_sb[:], in_=Wt.rearrange("(i p) d -> p i d", p=P))
         load_query(1)
         load_query(2)
         load_query(3)
-        nc.sync.dma_start(out=bias_sb[:], in_=bt.partition_broadcast(P))
 
         ident_f32 = keep.tile([P, P], F32)
         make_identity(nc, ident_f32[:])
@@ -144,6 +148,16 @@ def tile_gatedspatialattentionlayer_pc_kernel(tc, adj, query, Wt, bt, out):
                 scales=w_scales[:],
                 in_=w_grouped[:].rearrange("p i o j -> p (i o j)"),
             )
+
+        bias_banks = []
+
+        def spread_bias():
+            bias_bank = psum.tile([P, FEATS], F32, tag="bank", name="bias_bank")
+            nc.tensor.matmul(out=bias_bank[:], lhsT=ones[:], rhs=bias_rows[:], start=True, stop=True)
+            bias_banks.append(bias_bank)
+
+        def keep_bias():
+            nc.scalar.copy(out=bias_sb[:], in_=bias_banks[0][:])
 
         q_grouped = keep.tile([P, GRAPHS, FEATS, PACK], BF16, align_bytes=64)
         q_codes = keep.tile([P, GRAPHS, FEATS], U32, align_bytes=64)
@@ -261,8 +275,10 @@ def tile_gatedspatialattentionlayer_pc_kernel(tc, adj, query, Wt, bt, out):
         normalise(2)
         normalise_diagonal(1)
         transpose_nadj(1)
+        spread_bias()
         group_query(0)
         group_nadj(1)
+        keep_bias()
         invert_sum(3)
         transpose_wt(0)
         transpose_wt(1)

import concourse.mybir as mybir
from concourse.masks import make_identity

FP8X4 = mybir.dt.float8_e4m3fn_x4
BF16 = mybir.dt.bfloat16
F32 = mybir.dt.float32
U32 = mybir.dt.uint32
U8 = mybir.dt.uint8
ALU = mybir.AluOpType
ACT = mybir.ActivationFunctionType

P = 128
PACK = 4
NODES = 512
FEATS = 512
GRAPHS = 4
TILES = NODES // P
UNITS = GRAPHS * TILES
FLT_MAX = 3.4028234663852886e38
GPSIMD_COLS = 384
FIRST_SHARED_RELU = 4

FLOPS = 2 * 2 * GRAPHS * NODES * NODES * FEATS


def words(ap, pattern, **sizes):
    return ap.rearrange("p a b -> p (a b)").bitcast(F32).rearrange(pattern, **sizes)


def tile_gatedspatialattentionlayer_pc_kernel(tc, adj, query, Wt, bt, out):
    nc = tc.nc
    query_rows = query.flatten_outer_dims()
    out_rows = out.flatten_outer_dims()

    with tc.tile_pool(name="keep", bufs=1) as keep, tc.tile_pool(
        name="work", bufs=UNITS
    ) as work, tc.psum_pool(name="psum", bufs=8) as psum, tc.manual_schedule():

        adj_sb = keep.tile([P, TILES, NODES], BF16)
        query_sb = keep.tile([P, GRAPHS, PACK, FEATS], BF16)
        wt_sb = keep.tile([P, TILES, FEATS], BF16)
        bias_rows = keep.tile([P, FEATS], BF16)
        bias_sb = keep.tile([P, FEATS], BF16)
        ones = keep.tile([P, P], BF16)
        nc.vector.memset(bias_rows[:], 0.0)
        nc.vector.memset(ones[:], 1.0)

        def load_query(g):
            nc.sync.dma_start(
                out=query_sb[:, g, :, :].rearrange("p (u e) d -> p u (e d)", u=2),
                in_=query_rows[g * NODES : (g + 1) * NODES, :].rearrange(
                    "(u p e) d -> p u (e d)", u=2, e=2
                ),
            )

        for i in range(TILES):
            nc.sync.dma_start(out=adj_sb[:, i, :], in_=adj[i * P : (i + 1) * P, :])
        load_query(0)
        nc.sync.dma_start(out=bias_rows[:1, :], in_=bt.rearrange("(a d) -> a d", a=1))
        nc.sync.dma_start(out=wt_sb[:], in_=Wt.rearrange("(i p) d -> p i d", p=P))
        load_query(1)
        load_query(2)
        load_query(3)

        ident_f32 = keep.tile([P, P], F32)
        make_identity(nc, ident_f32[:])

        row_sum = keep.tile([P, TILES], F32)
        inv_sum = keep.tile([P, TILES], F32)
        a_diag = keep.tile([P, TILES, P], F32)
        a_grouped = keep.tile([P, TILES, P, PACK], BF16, align_bytes=64)
        a_codes = keep.tile([P, NODES], U32, align_bytes=64)
        a_scales = keep.tile([P, NODES], U8, align_bytes=64)
        nadjs, a_banks = {}, {}

        def sum_row(i):
            unused = work.tile([P, NODES], BF16, tag="unused")
            nc.scalar.activation(
                out=unused[:],
                in_=adj_sb[:, i, :],
                func=ACT.Copy,
                bias=1.0 / NODES,
                accum_out=row_sum[:, i : i + 1],
            )

        def add_self_loops(i):
            nc.vector.tensor_tensor(
                out=a_diag[:, i, :], in0=adj_sb[:, i, i * P : (i + 1) * P], in1=ident_f32[:], op=ALU.add
            )

        def invert_sum(i):
            nc.vector.reciprocal(out=inv_sum[:, i : i + 1], in_=row_sum[:, i : i + 1])

        def normalise(i):
            nadjs[i] = work.tile([P, NODES], BF16, tag="nadj", name="nadj")
            nc.vector.tensor_scalar_mul(out=nadjs[i][:], in0=adj_sb[:, i, :], scalar1=inv_sum[:, i : i + 1])

        def normalise_diagonal(i):
            nc.vector.tensor_scalar_mul(
                out=nadjs[i][:, i * P : (i + 1) * P], in0=a_diag[:, i, :], scalar1=inv_sum[:, i : i + 1]
            )

        def transpose_nadj(i):
            a_bank = psum.tile([P, 2, P], F32, tag="bank", name="a_bank")
            nadj_words = nadjs[i][:].bitcast(F32)
            for u in range(2):
                nc.tensor.transpose(
                    out=a_bank[:, u, :], in_=nadj_words[:, u * P : (u + 1) * P], identity=ident_f32[:]
                )
            a_banks[i] = a_bank

        def group_nadj(i):
            nc.scalar.copy(
                out=words(a_grouped[:, i, :, :], "p (n u) -> p n u", u=2),
                in_=a_banks[i][:].rearrange("p u n -> p n u"),
            )

        def quantise_nadj(i):
            nc.vector.quantize_mx(
                out=a_codes[:, i * P : (i + 1) * P].bitcast(FP8X4),
                scales=a_scales[:, i * P : (i + 1) * P],
                in_=a_grouped[:, i, :, :].rearrange("p n j -> p (n j)"),
            )

        w_grouped = keep.tile([P, TILES, P, PACK], BF16, align_bytes=64)
        w_codes = keep.tile([P, FEATS], U32, align_bytes=64)
        w_scales = keep.tile([P, FEATS], U8, align_bytes=64)
        w_banks = {}

        def transpose_wt(i):
            w_bank = psum.tile([P, 2, P], F32, tag="bank", name="w_bank")
            wt_words = wt_sb[:, i, :].bitcast(F32)
            for u in range(2):
                nc.tensor.transpose(
                    out=w_bank[:, u, :], in_=wt_words[:, u * P : (u + 1) * P], identity=ident_f32[:]
                )
            w_banks[i] = w_bank

        def group_wt(i, engine_copy):
            engine_copy(
                out=words(w_grouped[:, i, :, :], "p (o u) -> p o u", u=2),
                in_=w_banks[i][:].rearrange("p u o -> p o u"),
            )

        def quantise_wt():
            nc.vector.quantize_mx(
                out=w_codes[:].bitcast(FP8X4),
                scales=w_scales[:],
                in_=w_grouped[:].rearrange("p i o j -> p (i o j)"),
            )

        bias_banks = []

        def spread_bias():
            bias_bank = psum.tile([P, FEATS], F32, tag="bank", name="bias_bank")
            nc.tensor.matmul(out=bias_bank[:], lhsT=ones[:], rhs=bias_rows[:], start=True, stop=True)
            bias_banks.append(bias_bank)

        def keep_bias():
            nc.scalar.copy(out=bias_sb[:], in_=bias_banks[0][:])

        q_grouped = keep.tile([P, GRAPHS, FEATS, PACK], BF16, align_bytes=64)
        q_codes = keep.tile([P, GRAPHS, FEATS], U32, align_bytes=64)
        q_scales = keep.tile([P, GRAPHS, FEATS], U8, align_bytes=64)

        def group_query(g):
            group_part_of_query(nc.vector.tensor_copy, g, 0, 2 * P)

        def group_part_of_query(engine_copy, g, first, count):
            part = slice(first // 2, (first + count) // 2)
            engine_copy(
                out=q_grouped[:, g, :, :].rearrange("p (e q r) j -> p q j e r", e=2, r=2)[:, part],
                in_=query_sb[:, g, :, :].rearrange("p j (q r e) -> p q j e r", r=2, e=2)[:, part],
            )

        def group_half_query(g):
            group_part_of_query(nc.vector.tensor_copy, g, P, P)

        def group_query_on_scalar(g, k):
            group_part_of_query(nc.scalar.copy, g, k * (P // 2), P // 2)

        def quantise_query(g):
            nc.vector.quantize_mx(
                out=q_codes[:, g, :].bitcast(FP8X4),
                scales=q_scales[:, g, :],
                in_=q_grouped[:, g, :, :].rearrange("p d j -> p (d j)"),
            )

        gq_banks, gq_groupeds, out_banks, biaseds = {}, {}, {}, {}

        def first_product(u):
            g, cols = u // TILES, slice((u % TILES) * P, (u % TILES + 1) * P)
            gq_bank = psum.tile([P, PACK, P], F32, tag="bank", name="gq_bank")
            for j in range(PACK):
                block = slice((2 * (j % 2) + j // 2) * P, (2 * (j % 2) + j // 2 + 1) * P)
                nc.tensor.matmul_mx(
                    out=gq_bank[:, j, :],
                    lhsT=q_codes[:, g, block].bitcast(FP8X4),
                    lhsT_scale=q_scales[:, g, block],
                    rhs=a_codes[:, cols].bitcast(FP8X4),
                    rhs_scale=a_scales[:, cols],
                    start=True,
                    stop=True,
                )
            gq_banks[u] = gq_bank

        def round_gq(u):
            gq_grouped = work.tile([P, P, PACK], BF16, tag="gq_grouped", align_bytes=64)
            nc.scalar.copy(out=gq_grouped[:], in_=gq_banks[u][:].rearrange("p j n -> p n j"))
            gq_groupeds[u] = gq_grouped

        def second_product(u):
            gq_codes = work.tile([P, P], U32, tag="gq_codes", align_bytes=64)
            gq_scales = work.tile([P, P], U8, tag="gq_scales", align_bytes=64)
            nc.vector.quantize_mx(
                out=gq_codes[:].bitcast(FP8X4),
                scales=gq_scales[:],
                in_=gq_groupeds[u][:].rearrange("p n j -> p (n j)"),
            )
            out_bank = psum.tile([P, FEATS], F32, tag="bank", name="out_bank")
            nc.tensor.matmul_mx(
                out=out_bank[:],
                lhsT=gq_codes[:].bitcast(FP8X4),
                lhsT_scale=gq_scales[:],
                rhs=w_codes[:].bitcast(FP8X4),
                rhs_scale=w_scales[:],
                start=True,
                stop=True,
            )
            out_banks[u] = out_bank

        def add_bias(u):
            biased = work.tile([P, FEATS], F32, tag="biased")
            nc.vector.tensor_tensor(out=biased[:], in0=out_banks[u][:], in1=bias_sb[:], op=ALU.add)
            biaseds[u] = biased

        def relu_and_store(u):
            biased = biaseds[u]
            result = work.tile([P, FEATS], F32, tag="result")
            if u == UNITS - 1:
                half = slice(0, FEATS // 2), slice(FEATS // 2, FEATS)
                nc.vector.tensor_scalar_max(out=result[:, half[0]], in0=biased[:, half[0]], scalar1=0.0)
                nc.scalar.activation(out=result[:, half[1]], in_=biased[:, half[1]], func=ACT.Relu)
            else:
                cols = FEATS if u < FIRST_SHARED_RELU else 0 if u == UNITS - 2 else GPSIMD_COLS
                if cols > 0:
                    nc.gpsimd.tensor_scalar(
                        out=result[:, :cols],
                        in0=biased[:, :cols],
                        scalar1=FLT_MAX,
                        scalar2=0.0,
                        op0=ALU.min,
                        op1=ALU.max,
                    )
                if cols < FEATS:
                    nc.scalar.activation(out=result[:, cols:], in_=biased[:, cols:], func=ACT.Relu)
            nc.sync.dma_start(out=out_rows[u * P : (u + 1) * P, :], in_=result[:])

        sum_row(0)
        sum_row(1)
        add_self_loops(0)
        add_self_loops(1)
        invert_sum(0)
        normalise(0)
        add_self_loops(2)
        sum_row(2)
        add_self_loops(3)
        invert_sum(1)
        normalise_diagonal(0)
        transpose_nadj(0)
        sum_row(3)
        invert_sum(2)
        normalise(1)
        group_nadj(0)
        normalise(2)
        normalise_diagonal(1)
        transpose_nadj(1)
        spread_bias()
        group_query(0)
        group_nadj(1)
        keep_bias()
        invert_sum(3)
        transpose_wt(0)
        transpose_wt(1)
        quantise_nadj(0)
        normalise_diagonal(2)
        transpose_nadj(2)
        transpose_wt(2)
        transpose_wt(3)
        normalise(3)
        group_wt(0, nc.scalar.copy)
        group_wt(1, nc.scalar.copy)
        quantise_query(0)
        first_product(0)
        quantise_nadj(1)
        first_product(1)
        group_nadj(2)
        group_wt(2, nc.scalar.copy)
        normalise_diagonal(3)
        transpose_nadj(3)
        round_gq(0)
        group_wt(3, nc.scalar.copy)
        group_nadj(3)
        group_query(1)
        round_gq(1)
        quantise_nadj(2)
        first_product(2)
        quantise_wt()
        quantise_query(1)
        quantise_nadj(3)
        first_product(3)

        for step in range(UNITS + 3):
            if 4 <= step + 1 < UNITS:
                first_product(step + 1)
            if 2 <= step < UNITS:
                round_gq(step)
            if 1 <= step <= 2:
                group_query_on_scalar(2, step - 1)
            if 4 <= step <= 7:
                group_query_on_scalar(3, step - 4)
            if 0 <= step - 2 < UNITS:
                second_product(step - 2)
            if 0 <= step - 3 < UNITS:
                add_bias(step - 3)
            if FIRST_SHARED_RELU <= step - 4 < UNITS - 1:
                relu_and_store(step - 4)
            if 0 <= step - 3 < FIRST_SHARED_RELU or step - 3 == UNITS - 1:
                relu_and_store(step - 3)
            if step == 2:
                group_half_query(2)
            if step == 5:
                quantise_query(2)
            if step == 9:
                quantise_query(3)
